import numpy as np
import ml_dtypes


def mxq(x, axis, fmt="e4m3"):
    dtype, down = {"e4m3": (ml_dtypes.float8_e4m3fn, 7), "e5m2": (ml_dtypes.float8_e5m2, 14)}[fmt]
    v = np.moveaxis(np.asarray(x, np.float32).astype(ml_dtypes.bfloat16).astype(np.float64), axis, -1)
    blocks = v.reshape(v.shape[:-1] + (-1, 32))
    amax = np.abs(blocks).max(-1, keepdims=True)
    byte = np.maximum(np.where(amax > 0, np.frexp(amax)[1] - 1 + 127, 0) - down, 1)
    scale = np.exp2(byte - 127.0)
    codes = (blocks / scale).astype(np.float32).astype(dtype).astype(np.float64)
    return np.moveaxis((codes * scale).reshape(v.shape), -1, axis)


WIDE = False


def mx_kscale(k):
    if not WIDE:
        return np.ones(k)
    levels = np.array([10, -10, 5, -5, 0])
    if k % 512:
        return np.exp2(np.random.permutation(np.resize(levels, k // 32))).repeat(32)
    a = np.empty((k // 512, 16))
    for p in range(k // 512):
        a[p, :8] = np.random.permutation(np.resize(levels, 8))
        for g in range(8):
            far = levels[np.abs(levels - a[p, g]) >= 10]
            a[p, g + 8] = far[np.random.randint(len(far))]
    return np.exp2(a.ravel()).repeat(32)


BF16 = ml_dtypes.bfloat16


def bf(x):
    return np.asarray(x, np.float32).astype(BF16)


def f64(x):
    return np.asarray(x).astype(np.float64)


B, N, DIM, HEADS, DIM_HEAD = 2, 512, 1024, 16, 64
INNER = HEADS * DIM_HEAD


def setup_inputs():
    s = mx_kscale(DIM)
    return {"x": bf(np.random.standard_normal((B, N, DIM)) * s),
            "W": bf(np.random.standard_normal((3 * INNER, DIM)) / np.sqrt(DIM) / s[None, :])}


def reference(x, W):
    b, n, _ = x.shape
    qkv = mxq(f64(x), 2, "e4m3") @ mxq(f64(W), 1, "e4m3").T
    q, k, v = np.split(qkv, 3, axis=-1)

    def to_heads(t):
        return t.reshape(b, n, HEADS, DIM_HEAD).transpose(0, 2, 1, 3)

    return to_heads(q), to_heads(k), to_heads(v)

@@ -1,0 +1,195 @@
+from contextlib import ExitStack
+
+import concourse.mybir as mybir
+from concourse.masks import make_identity
+
+F32 = mybir.dt.float32
+BF16 = mybir.dt.bfloat16
+U32 = mybir.dt.uint32
+U8 = mybir.dt.uint8
+FP8X4 = mybir.dt.float8_e4m3fn_x4
+
+P = 128
+K = 1024
+TOK = 1024
+E = 3072
+FLOPS = 2 * TOK * K * E
+
+SETS = 8
+WBLK = 6
+V = 0
+S = 1
+
+
+def tile_get_qkv_kernel(tc, x, W, out_0, out_1, out_2):
+    nc = tc.nc
+    outs = [out_0, out_1, out_2]
+    with ExitStack() as ctx:
+        keep = ctx.enter_context(tc.tile_pool(name="keep", bufs=1))
+        rot = ctx.enter_context(tc.tile_pool(name="rot", bufs=3))
+        psum = ctx.enter_context(tc.psum_pool(name="psum", bufs=1))
+        ctx.enter_context(tc.manual_schedule())
+
+        counter = [0]
+
+        def new_bank():
+            i = counter[0] % 8
+            counter[0] += 1
+            return psum.tile([P, 512], F32, name="bank%d" % i, tag="bank%d" % i)
+
+        x_sb = [keep.tile([P, 2 * K], BF16, name="x_sb%d" % i) for i in range(4)]
+        w_sb = {}
+
+        def load_x(part):
+            for b in range(2):
+                src = x[b].rearrange("(q s) k -> q (s k)", s=SETS)
+                nc.sync.dma_start(out=x_sb[part][b:P:2, :],
+                                  in_=src[:, part * 2 * K:(part + 1) * 2 * K])
+
+        def load_w(wb, pieces):
+            rows = W[wb * 512:(wb + 1) * 512, :].rearrange("(p t) k -> p (t k)", t=4)
+            n = 4 // pieces
+            for i in range(pieces):
+                w_t = keep.tile([P, n * K], BF16, name="w_sb%d_%d" % (wb, i))
+                nc.sync.dma_start(out=w_t[:], in_=rows[:, i * n * K:(i + 1) * n * K])
+                for j in range(n):
+                    w_sb[(wb, i * n + j)] = w_t[:].bitcast(F32)[:, j * 512:(j + 1) * 512]
+
+        load_x(0)
+        load_w(0, 2)
+        load_x(1)
+        load_x(2)
+        load_x(3)
+        for wb in range(1, WBLK):
+            load_w(wb, 1)
+
+        ident = keep.tile([P, P], F32, name="ident")
+        make_identity(nc, ident[:])
+
+        xg = [keep.tile([P, 2 * K], BF16, name="xg%d" % i, align_bytes=64) for i in range(4)]
+        x_codes = [keep.tile([P, 512], U32, name="x_codes%d" % i, align_bytes=64) for i in range(4)]
+        x_scales = [keep.tile([P, 512], U8, name="x_scales%d" % i, align_bytes=64) for i in range(4)]
+
+        def copy(eng, dst, src):
+            if eng == V:
+                nc.vector.tensor_copy(out=dst, in_=src)
+            else:
+                nc.scalar.copy(out=dst, in_=src)
+
+        def transpose4(words):
+            bank = new_bank()
+            for j in range(4):
+                w0 = 256 * (j // 2) + j % 2
+                nc.tensor.transpose(bank[:, j * P:(j + 1) * P], words[:, w0:w0 + 255:2], ident[:])
+            return bank
+
+        def transpose_x(s, eng):
+            bank = transpose4(x_sb[s // 2][:].bitcast(F32)[:, (s % 2) * 512:(s % 2 + 1) * 512])
+            dst = xg[s // 2][:].bitcast(F32)[:, (s % 2) * 512:(s % 2 + 1) * 512]
+            copy(eng, dst.rearrange("p (g c u) -> p g c u", g=2, u=2),
+                 bank[:].rearrange("p (g u c) -> p g c u", g=2, u=2))
+
+        def quantise_x(part):
+            nc.vector.quantize_mx(out=x_codes[part][:].bitcast(FP8X4), scales=x_scales[part][:],
+                                  in_=xg[part][:])
+
+        w_codes = {}
+        w_scales = {}
+        w_grouped = {}
+
+        def transpose_w(wb, engines, q_calls):
+            wg = rot.tile([P, 4096], BF16, name="wg", tag="wg", align_bytes=64)
+            wg32 = wg[:].bitcast(F32).rearrange(
+                "p (g a t c u) -> p g a t c u", g=2, a=2, t=4, c=64, u=2)
+            for t in range(4):
+                bank = transpose4(w_sb[(wb, t)])
+                copy(engines[t], wg32[:, :, :, t, :, :],
+                     bank[:].rearrange("p (g u a c) -> p g a c u", g=2, u=2, a=2, c=64))
+            w_codes[wb] = rot.tile([P, 1024], U32, name="wc", tag="wc", align_bytes=64)
+            w_scales[wb] = rot.tile([P, 1024], U8, name="ws", tag="ws", align_bytes=64)
+            w_grouped[wb] = wg
+            quantise_w(wb, q_calls)
+
+        def quantise_w(wb, q_calls):
+            for c0, n in q_calls:
+                nc.vector.quantize_mx(
+                    out=w_codes[wb][:, c0:c0 + n].bitcast(FP8X4),
+                    scales=w_scales[wb][:, c0:c0 + n],
+                    in_=w_grouped[wb][:, 4 * c0:4 * (c0 + n)],
+                )
+
+        def mx_pass(acc, s, g, wb, a):
+            off = (s % 2) * 256 + g * P
+            c0 = g * 512 + a * 256
+            nc.tensor.matmul_mx(
+                out=acc,
+                lhsT=x_codes[s // 2][:, off:off + P].bitcast(FP8X4),
+                lhsT_scale=x_scales[s // 2][:, off:off + P],
+                rhs=w_codes[wb][:, c0:c0 + 256].bitcast(FP8X4),
+                rhs_scale=w_scales[wb][:, c0:c0 + 256],
+                start=(g == 0),
+                stop=(g == 1),
+            )
+
+        o_sb = {}
+
+        def multiply(wb, a, pairs, engines):
+            if (wb, a) not in o_sb:
+                o_sb[(wb, a)] = keep.tile([P, 2048], F32, name="o_sb%d_%d" % (wb, a))
+            o_view = o_sb[(wb, a)][:].rearrange(
+                "p (h s q t) -> p s h q t", h=4, s=SETS, q=16, t=4)
+            for n, pair in enumerate(pairs):
+                acc = new_bank()
+                for i in range(2):
+                    for g in range(2):
+                        mx_pass(acc[:, i * 256:(i + 1) * 256], 2 * pair + i, g, wb, a)
+                copy(engines[n], o_view[:, 2 * pair:2 * pair + 2, :, :, :],
+                     acc[:].rearrange("p (i t h q) -> p i h q t", i=2, t=4, h=4, q=16))
+
+        def store(wb, a, s0, s1):
+            h0 = (wb % 2) * 8 + a * 4
+            for b in range(2):
+                dst = outs[wb // 2][b, h0:h0 + 4].rearrange("h (q s) d -> q h s d", s=SETS)
+                src = o_sb[(wb, a)][b:P:2, :].rearrange("p (h s d) -> p h s d", h=4, s=SETS)
+                nc.sync.dma_start(out=dst[:, :, s0:s1, :], in_=src[:, :, s0:s1, :])
+
+        QUARTERS = [(0, 256), (512, 256), (256, 256), (768, 256)]
+        HALVES = [(0, 512), (512, 512)]
+
+        def block(wb, engines):
+            for a in range(2):
+                multiply(wb, a, [0, 1, 2, 3], engines)
+                store(wb, a, 0, SETS)
+
+        transpose_x(0, V)
+        transpose_x(1, S)
+        quantise_x(0)
+        transpose_w(0, [V, S, V, S], QUARTERS[0:2])
+        transpose_x(2, V)
+        transpose_x(3, S)
+        quantise_w(0, QUARTERS[2:4])
+        quantise_x(1)
+        transpose_x(4, S)
+        transpose_x(5, S)
+        multiply(0, 0, [0], [S])
+        multiply(0, 1, [0], [S])
+        transpose_x(6, V)
+        transpose_x(7, V)
+        multiply(0, 0, [1], [S])
+        multiply(0, 1, [1], [S])
+        quantise_x(2)
+        quantise_x(3)
+        transpose_w(1, [V, V, S, S], QUARTERS)
+        multiply(0, 0, [2, 3], [S, S])
+        store(0, 0, 0, SETS)
+        multiply(0, 1, [2, 3], [S, S])
+        store(0, 1, 0, SETS)
+        transpose_w(2, [V, V, V, V], HALVES)
+        transpose_w(3, [V, V, V, V], HALVES)
+        block(1, [S, S, S, S])
+        block(2, [S, S, S, V])
+        transpose_w(4, [V, V, V, V], HALVES)
+        transpose_w(5, [V, V, V, V], HALVES)
+        block(3, [S, S, S, S])
+        block(4, [S, S, S, V])
+        block(5, [S, V, S, V])

@@ -27,6 +27,7 @@ def tile_get_qkv_kernel(tc, x, W, out_0, out_1, out_2):
     with ExitStack() as ctx:
         keep = ctx.enter_context(tc.tile_pool(name="keep", bufs=1))
         rot = ctx.enter_context(tc.tile_pool(name="rot", bufs=3))
+        outp = ctx.enter_context(tc.tile_pool(name="outp", bufs=8))
         psum = ctx.enter_context(tc.psum_pool(name="psum", bufs=1))
         ctx.enter_context(tc.manual_schedule())
 
@@ -39,6 +40,7 @@ def tile_get_qkv_kernel(tc, x, W, out_0, out_1, out_2):
 
         x_sb = [keep.tile([P, 2 * K], BF16, name="x_sb%d" % i) for i in range(4)]
         w_sb = {}
+        w_raw = {}
 
         def load_x(part):
             for b in range(2):
@@ -52,6 +54,7 @@ def tile_get_qkv_kernel(tc, x, W, out_0, out_1, out_2):
             for i in range(pieces):
                 w_t = keep.tile([P, n * K], BF16, name="w_sb%d_%d" % (wb, i))
                 nc.sync.dma_start(out=w_t[:], in_=rows[:, i * n * K:(i + 1) * n * K])
+                w_raw[wb] = w_t
                 for j in range(n):
                     w_sb[(wb, i * n + j)] = w_t[:].bitcast(F32)[:, j * 512:(j + 1) * 512]
 
@@ -76,15 +79,19 @@ def tile_get_qkv_kernel(tc, x, W, out_0, out_1, out_2):
             else:
                 nc.scalar.copy(out=dst, in_=src)
 
-        def transpose4(words):
+        def transpose4(words, ordered):
             bank = new_bank()
             for j in range(4):
-                w0 = 256 * (j // 2) + j % 2
-                nc.tensor.transpose(bank[:, j * P:(j + 1) * P], words[:, w0:w0 + 255:2], ident[:])
+                if ordered:
+                    src = words[:, j * P:(j + 1) * P]
+                else:
+                    w0 = 256 * (j // 2) + j % 2
+                    src = words[:, w0:w0 + 255:2]
+                nc.tensor.transpose(bank[:, j * P:(j + 1) * P], src, ident[:])
             return bank
 
         def transpose_x(s, eng):
-            bank = transpose4(x_sb[s // 2][:].bitcast(F32)[:, (s % 2) * 512:(s % 2 + 1) * 512])
+            bank = transpose4(x_sb[s // 2][:].bitcast(F32)[:, (s % 2) * 512:(s % 2 + 1) * 512], False)
             dst = xg[s // 2][:].bitcast(F32)[:, (s % 2) * 512:(s % 2 + 1) * 512]
             copy(eng, dst.rearrange("p (g c u) -> p g c u", g=2, u=2),
                  bank[:].rearrange("p (g u c) -> p g c u", g=2, u=2))
@@ -97,18 +104,31 @@ def tile_get_qkv_kernel(tc, x, W, out_0, out_1, out_2):
         w_scales = {}
         w_grouped = {}
 
-        def transpose_w(wb, engines, q_calls):
+        w_ordered = {}
+
+        def order_w(wb):
+            wo = rot.tile([P, 2048], F32, name="wo", tag="wo")
+            w_ordered[wb] = wo
+            src = w_raw[wb][:].bitcast(F32)
+            for h in range(2):
+                nc.vector.tensor_copy(
+                    out=wo[:, h * 1024:(h + 1) * 1024].rearrange("p (m u c) -> p m u c", m=4, u=2),
+                    in_=src[:, h * 1024:(h + 1) * 1024].rearrange("p (m c u) -> p m u c", m=4, u=2))
+
+        def transpose_w(wb, engines):
             wg = rot.tile([P, 4096], BF16, name="wg", tag="wg", align_bytes=64)
             wg32 = wg[:].bitcast(F32).rearrange(
                 "p (g a t c u) -> p g a t c u", g=2, a=2, t=4, c=64, u=2)
             for t in range(4):
-                bank = transpose4(w_sb[(wb, t)])
+                if wb in w_ordered:
+                    bank = transpose4(w_ordered[wb][:, t * 512:(t + 1) * 512], True)
+                else:
+                    bank = transpose4(w_sb[(wb, t)], False)
                 copy(engines[t], wg32[:, :, :, t, :, :],
                      bank[:].rearrange("p (g u a c) -> p g a c u", g=2, u=2, a=2, c=64))
             w_codes[wb] = rot.tile([P, 1024], U32, name="wc", tag="wc", align_bytes=64)
             w_scales[wb] = rot.tile([P, 1024], U8, name="ws", tag="ws", align_bytes=64)
             w_grouped[wb] = wg
-            quantise_w(wb, q_calls)
 
         def quantise_w(wb, q_calls):
             for c0, n in q_calls:
@@ -135,7 +155,7 @@ def tile_get_qkv_kernel(tc, x, W, out_0, out_1, out_2):
 
         def multiply(wb, a, pairs, engines):
             if (wb, a) not in o_sb:
-                o_sb[(wb, a)] = keep.tile([P, 2048], F32, name="o_sb%d_%d" % (wb, a))
+                o_sb[(wb, a)] = outp.tile([P, 2048], F32, name="o_sb", tag="o_sb")
             o_view = o_sb[(wb, a)][:].rearrange(
                 "p (h s q t) -> p s h q t", h=4, s=SETS, q=16, t=4)
             for n, pair in enumerate(pairs):
@@ -156,15 +176,11 @@ def tile_get_qkv_kernel(tc, x, W, out_0, out_1, out_2):
         QUARTERS = [(0, 256), (512, 256), (256, 256), (768, 256)]
         HALVES = [(0, 512), (512, 512)]
 
-        def block(wb, engines):
-            for a in range(2):
-                multiply(wb, a, [0, 1, 2, 3], engines)
-                store(wb, a, 0, SETS)
-
         transpose_x(0, V)
         transpose_x(1, S)
         quantise_x(0)
-        transpose_w(0, [V, S, V, S], QUARTERS[0:2])
+        transpose_w(0, [V, S, V, S])
+        quantise_w(0, QUARTERS[0:2])
         transpose_x(2, V)
         transpose_x(3, S)
         quantise_w(0, QUARTERS[2:4])
@@ -179,17 +195,21 @@ def tile_get_qkv_kernel(tc, x, W, out_0, out_1, out_2):
         multiply(0, 1, [1], [S])
         quantise_x(2)
         quantise_x(3)
-        transpose_w(1, [V, V, S, S], QUARTERS)
-        multiply(0, 0, [2, 3], [S, S])
-        store(0, 0, 0, SETS)
-        multiply(0, 1, [2, 3], [S, S])
-        store(0, 1, 0, SETS)
-        transpose_w(2, [V, V, V, V], HALVES)
-        transpose_w(3, [V, V, V, V], HALVES)
-        block(1, [S, S, S, S])
-        block(2, [S, S, S, V])
-        transpose_w(4, [V, V, V, V], HALVES)
-        transpose_w(5, [V, V, V, V], HALVES)
-        block(3, [S, S, S, S])
-        block(4, [S, S, S, V])
-        block(5, [S, V, S, V])
+        order_w(1)
+        order_w(2)
+        for a in range(2):
+            multiply(0, a, [2, 3], [S, S])
+            store(0, a, 0, SETS)
+        transpose_w(1, [V, S, V, S])
+        quantise_w(1, HALVES)
+        transpose_w(2, [S, S, V, V])
+        for wb in range(1, WBLK):
+            if wb + 2 < WBLK:
+                order_w(wb + 2)
+            for a in range(2):
+                multiply(wb, a, [0, 1, 2, 3], [S, V, S, S] if wb + 2 < WBLK else [S, V, S, V])
+                store(wb, a, 0, SETS)
+                if a == 0 and wb + 1 < WBLK:
+                    quantise_w(wb + 1, HALVES)
+            if wb + 2 < WBLK:
+                transpose_w(wb + 2, [V, S, V, S])

@@ -83,7 +83,8 @@ def tile_get_qkv_kernel(tc, x, W, out_0, out_1, out_2):
             bank = new_bank()
             for j in range(4):
                 if ordered:
-                    src = words[:, j * P:(j + 1) * P]
+                    w0 = 512 * (j % 2) + P * (j // 2)
+                    src = words[:, w0:w0 + P]
                 else:
                     w0 = 256 * (j // 2) + j % 2
                     src = words[:, w0:w0 + 255:2]
@@ -112,8 +113,8 @@ def tile_get_qkv_kernel(tc, x, W, out_0, out_1, out_2):
             src = w_raw[wb][:].bitcast(F32)
             for h in range(2):
                 nc.vector.tensor_copy(
-                    out=wo[:, h * 1024:(h + 1) * 1024].rearrange("p (m u c) -> p m u c", m=4, u=2),
-                    in_=src[:, h * 1024:(h + 1) * 1024].rearrange("p (m c u) -> p m u c", m=4, u=2))
+                    out=wo[:, h * 1024:(h + 1) * 1024].rearrange("p (u c i) -> p c u i", u=2, i=4),
+                    in_=src[:, h * 1024:(h + 1) * 1024].rearrange("p (c i u) -> p c u i", i=4, u=2))
 
         def transpose_w(wb, engines):
             wg = rot.tile([P, 4096], BF16, name="wg", tag="wg", align_bytes=64)
@@ -121,7 +122,8 @@ def tile_get_qkv_kernel(tc, x, W, out_0, out_1, out_2):
                 "p (g a t c u) -> p g a t c u", g=2, a=2, t=4, c=64, u=2)
             for t in range(4):
                 if wb in w_ordered:
-                    bank = transpose4(w_ordered[wb][:, t * 512:(t + 1) * 512], True)
+                    h0 = (t // 2) * 1024 + (t % 2) * 256
+                    bank = transpose4(w_ordered[wb][:, h0:h0 + 768], True)
                 else:
                     bank = transpose4(w_sb[(wb, t)], False)
                 copy(engines[t], wg32[:, :, :, t, :, :],

@@ -38,15 +38,21 @@ def tile_get_qkv_kernel(tc, x, W, out_0, out_1, out_2):
             counter[0] += 1
             return psum.tile([P, 512], F32, name="bank%d" % i, tag="bank%d" % i)
 
-        x_sb = [keep.tile([P, 2 * K], BF16, name="x_sb%d" % i) for i in range(4)]
+        x_sb = [keep.tile([P, K], BF16, name="x_sb%d" % i) for i in range(2)]
+        x_sb += [keep.tile([P, 2 * K], BF16, name="x_sb%d" % i) for i in range(2, 5)]
         w_sb = {}
         w_raw = {}
 
-        def load_x(part):
+        def load_x(i):
+            s0, n = (i, 1) if i < 2 else (2 * i - 2, 2)
             for b in range(2):
                 src = x[b].rearrange("(q s) k -> q (s k)", s=SETS)
-                nc.sync.dma_start(out=x_sb[part][b:P:2, :],
-                                  in_=src[:, part * 2 * K:(part + 1) * 2 * K])
+                nc.sync.dma_start(out=x_sb[i][b:P:2, :], in_=src[:, s0 * K:(s0 + n) * K])
+
+        def x_words(s):
+            if s < 2:
+                return x_sb[s][:].bitcast(F32)
+            return x_sb[s // 2 + 1][:].bitcast(F32)[:, (s % 2) * 512:(s % 2 + 1) * 512]
 
         def load_w(wb, pieces):
             rows = W[wb * 512:(wb + 1) * 512, :].rearrange("(p t) k -> p (t k)", t=4)
@@ -59,10 +65,11 @@ def tile_get_qkv_kernel(tc, x, W, out_0, out_1, out_2):
                     w_sb[(wb, i * n + j)] = w_t[:].bitcast(F32)[:, j * 512:(j + 1) * 512]
 
         load_x(0)
-        load_w(0, 2)
         load_x(1)
+        load_w(0, 2)
         load_x(2)
         load_x(3)
+        load_x(4)
         for wb in range(1, WBLK):
             load_w(wb, 1)
 
@@ -92,7 +99,7 @@ def tile_get_qkv_kernel(tc, x, W, out_0, out_1, out_2):
             return bank
 
         def transpose_x(s, eng):
-            bank = transpose4(x_sb[s // 2][:].bitcast(F32)[:, (s % 2) * 512:(s % 2 + 1) * 512], False)
+            bank = transpose4(x_words(s), False)
             dst = xg[s // 2][:].bitcast(F32)[:, (s % 2) * 512:(s % 2 + 1) * 512]
             copy(eng, dst.rearrange("p (g c u) -> p g c u", g=2, u=2),
                  bank[:].rearrange("p (g u c) -> p g c u", g=2, u=2))
@@ -199,12 +206,13 @@ def tile_get_qkv_kernel(tc, x, W, out_0, out_1, out_2):
         quantise_x(3)
         order_w(1)
         order_w(2)
-        for a in range(2):
-            multiply(0, a, [2, 3], [S, S])
-            store(0, a, 0, SETS)
+        multiply(0, 0, [2, 3], [S, S])
+        store(0, 0, 0, SETS)
         transpose_w(1, [V, S, V, S])
+        multiply(0, 1, [2, 3], [S, S])
+        store(0, 1, 0, SETS)
         quantise_w(1, HALVES)
-        transpose_w(2, [S, S, V, V])
+        transpose_w(2, [S, V, S, V])
         for wb in range(1, WBLK):
             if wb + 2 < WBLK:
                 order_w(wb + 2)

@@ -66,7 +66,7 @@ def tile_get_qkv_kernel(tc, x, W, out_0, out_1, out_2):
 
         load_x(0)
         load_x(1)
-        load_w(0, 2)
+        load_w(0, 4)
         load_x(2)
         load_x(3)
         load_x(4)
@@ -198,12 +198,12 @@ def tile_get_qkv_kernel(tc, x, W, out_0, out_1, out_2):
         transpose_x(5, S)
         multiply(0, 0, [0], [S])
         multiply(0, 1, [0], [S])
+        quantise_x(2)
         transpose_x(6, V)
-        transpose_x(7, V)
+        transpose_x(7, S)
+        quantise_x(3)
         multiply(0, 0, [1], [S])
         multiply(0, 1, [1], [S])
-        quantise_x(2)
-        quantise_x(3)
         order_w(1)
         order_w(2)
         multiply(0, 0, [2, 3], [S, S])
@@ -217,9 +217,9 @@ def tile_get_qkv_kernel(tc, x, W, out_0, out_1, out_2):
             if wb + 2 < WBLK:
                 order_w(wb + 2)
             for a in range(2):
-                multiply(wb, a, [0, 1, 2, 3], [S, V, S, S] if wb + 2 < WBLK else [S, V, S, V])
+                multiply(wb, a, [0, 1, 2, 3], [S, S, S, S] if wb + 1 < WBLK else [S, V, S, V])
                 store(wb, a, 0, SETS)
                 if a == 0 and wb + 1 < WBLK:
                     quantise_w(wb + 1, HALVES)
             if wb + 2 < WBLK:
-                transpose_w(wb + 2, [V, S, V, S])
+                transpose_w(wb + 2, [V, V, V, V])

@@ -17,6 +17,7 @@ FLOPS = 2 * TOK * K * E
 
 SETS = 8
 WBLK = 6
+CUT = [(4, 0), (4, 1), (5, 0), (5, 1)]
 V = 0
 S = 1
 
@@ -127,14 +128,24 @@ def tile_get_qkv_kernel(tc, x, W, out_0, out_1, out_2):
             wg = rot.tile([P, 4096], BF16, name="wg", tag="wg", align_bytes=64)
             wg32 = wg[:].bitcast(F32).rearrange(
                 "p (g a t c u) -> p g a t c u", g=2, a=2, t=4, c=64, u=2)
+            wg_cut = wg[:].bitcast(F32).rearrange(
+                "p (g a e t c u) -> p g a e t c u", g=2, a=2, e=2, t=4, c=32, u=2)
             for t in range(4):
                 if wb in w_ordered:
                     h0 = (t // 2) * 1024 + (t % 2) * 256
                     bank = transpose4(w_ordered[wb][:, h0:h0 + 768], True)
                 else:
                     bank = transpose4(w_sb[(wb, t)], False)
-                copy(engines[t], wg32[:, :, :, t, :, :],
-                     bank[:].rearrange("p (g u a c) -> p g a c u", g=2, u=2, a=2, c=64))
+                whole = bank[:].rearrange("p (g u a c) -> p g a c u", g=2, u=2, a=2, c=64)
+                if (wb, 0) not in CUT and (wb, 1) not in CUT:
+                    copy(engines[t], wg32[:, :, :, t, :, :], whole)
+                else:
+                    cut = bank[:].rearrange("p (g u a e c) -> p g a e c u", g=2, u=2, a=2, e=2, c=32)
+                    for a in range(2):
+                        if (wb, a) in CUT:
+                            copy(engines[t], wg_cut[:, :, a, :, t, :, :], cut[:, :, a, :, :, :])
+                        else:
+                            copy(engines[t], wg32[:, :, a, t, :, :], whole[:, :, a, :, :])
             w_codes[wb] = rot.tile([P, 1024], U32, name="wc", tag="wc", align_bytes=64)
             w_scales[wb] = rot.tile([P, 1024], U8, name="ws", tag="ws", align_bytes=64)
             w_grouped[wb] = wg
@@ -147,15 +158,15 @@ def tile_get_qkv_kernel(tc, x, W, out_0, out_1, out_2):
                     in_=w_grouped[wb][:, 4 * c0:4 * (c0 + n)],
                 )
 
-        def mx_pass(acc, s, g, wb, a):
+        def mx_pass(acc, s, g, wb, col, n):
             off = (s % 2) * 256 + g * P
-            c0 = g * 512 + a * 256
+            c0 = g * 512 + col
             nc.tensor.matmul_mx(
                 out=acc,
                 lhsT=x_codes[s // 2][:, off:off + P].bitcast(FP8X4),
                 lhsT_scale=x_scales[s // 2][:, off:off + P],
-                rhs=w_codes[wb][:, c0:c0 + 256].bitcast(FP8X4),
-                rhs_scale=w_scales[wb][:, c0:c0 + 256],
+                rhs=w_codes[wb][:, c0:c0 + n].bitcast(FP8X4),
+                rhs_scale=w_scales[wb][:, c0:c0 + n],
                 start=(g == 0),
                 stop=(g == 1),
             )
@@ -171,16 +182,33 @@ def tile_get_qkv_kernel(tc, x, W, out_0, out_1, out_2):
                 acc = new_bank()
                 for i in range(2):
                     for g in range(2):
-                        mx_pass(acc[:, i * 256:(i + 1) * 256], 2 * pair + i, g, wb, a)
+                        mx_pass(acc[:, i * 256:(i + 1) * 256], 2 * pair + i, g, wb, a * 256, 256)
                 copy(engines[n], o_view[:, 2 * pair:2 * pair + 2, :, :, :],
                      acc[:].rearrange("p (i t h q) -> p i h q t", i=2, t=4, h=4, q=16))
 
-        def store(wb, a, s0, s1):
-            h0 = (wb % 2) * 8 + a * 4
+        def store(wb, a):
+            store_heads(wb, a * 4, 4, o_sb[(wb, a)][:])
+
+        def store_heads(wb, h, heads, tile):
+            h0 = (wb % 2) * 8 + h
             for b in range(2):
-                dst = outs[wb // 2][b, h0:h0 + 4].rearrange("h (q s) d -> q h s d", s=SETS)
-                src = o_sb[(wb, a)][b:P:2, :].rearrange("p (h s d) -> p h s d", h=4, s=SETS)
-                nc.sync.dma_start(out=dst[:, :, s0:s1, :], in_=src[:, :, s0:s1, :])
+                nc.sync.dma_start(
+                    out=outs[wb // 2][b, h0:h0 + heads].rearrange("h (q s) d -> q h s d", s=SETS),
+                    in_=tile[b:P:2, :].rearrange("p (h s d) -> p h s d", h=heads, s=SETS))
+
+        def multiply_cut(wb, a, engines):
+            tile = outp.tile([P, 2048], F32, name="o_sb", tag="o_sb")
+            for e in range(2):
+                part = tile[:, e * 1024:(e + 1) * 1024]
+                o_view = part.rearrange("p (h s q t) -> p s h q t", h=2, s=SETS, q=16, t=4)
+                for n in range(2):
+                    acc = new_bank()
+                    for i in range(4):
+                        for g in range(2):
+                            mx_pass(acc[:, i * P:(i + 1) * P], 4 * n + i, g, wb, a * 256 + e * P, P)
+                    copy(engines[2 * e + n], o_view[:, 4 * n:4 * n + 4, :, :, :],
+                         acc[:].rearrange("p (i t h q) -> p i h q t", i=4, t=4, h=2, q=16))
+                store_heads(wb, a * 4 + 2 * e, 2, part)
 
         QUARTERS = [(0, 256), (512, 256), (256, 256), (768, 256)]
         HALVES = [(0, 512), (512, 512)]
@@ -207,18 +235,22 @@ def tile_get_qkv_kernel(tc, x, W, out_0, out_1, out_2):
         order_w(1)
         order_w(2)
         multiply(0, 0, [2, 3], [S, S])
-        store(0, 0, 0, SETS)
+        store(0, 0)
         transpose_w(1, [V, S, V, S])
         multiply(0, 1, [2, 3], [S, S])
-        store(0, 1, 0, SETS)
+        store(0, 1)
         quantise_w(1, HALVES)
         transpose_w(2, [S, V, S, V])
         for wb in range(1, WBLK):
             if wb + 2 < WBLK:
                 order_w(wb + 2)
             for a in range(2):
-                multiply(wb, a, [0, 1, 2, 3], [S, S, S, S] if wb + 1 < WBLK else [S, V, S, V])
-                store(wb, a, 0, SETS)
+                engines = [S, S, S, S] if wb + 1 < WBLK else [S, V, S, V]
+                if (wb, a) in CUT:
+                    multiply_cut(wb, a, engines)
+                else:
+                    multiply(wb, a, [0, 1, 2, 3], engines)
+                    store(wb, a)
                 if a == 0 and wb + 1 < WBLK:
                     quantise_w(wb + 1, HALVES)
             if wb + 2 < WBLK:

@@ -29,6 +29,7 @@ def tile_get_qkv_kernel(tc, x, W, out_0, out_1, out_2):
         keep = ctx.enter_context(tc.tile_pool(name="keep", bufs=1))
         rot = ctx.enter_context(tc.tile_pool(name="rot", bufs=3))
         outp = ctx.enter_context(tc.tile_pool(name="outp", bufs=8))
+        cutp = ctx.enter_context(tc.tile_pool(name="cutp", bufs=5))
         psum = ctx.enter_context(tc.psum_pool(name="psum", bufs=1))
         ctx.enter_context(tc.manual_schedule())
 
@@ -193,13 +194,13 @@ def tile_get_qkv_kernel(tc, x, W, out_0, out_1, out_2):
             h0 = (wb % 2) * 8 + h
             for b in range(2):
                 nc.sync.dma_start(
-                    out=outs[wb // 2][b, h0:h0 + heads].rearrange("h (q s) d -> q h s d", s=SETS),
-                    in_=tile[b:P:2, :].rearrange("p (h s d) -> p h s d", h=heads, s=SETS))
+                    out=outs[wb // 2][b, h0:h0 + heads].rearrange("h (q s) d -> q h (s d)", s=SETS),
+                    in_=tile[b:P:2, :])
 
         def multiply_cut(wb, a, engines):
-            tile = outp.tile([P, 2048], F32, name="o_sb", tag="o_sb")
             for e in range(2):
-                part = tile[:, e * 1024:(e + 1) * 1024]
+                tile = cutp.tile([P, 1024], F32, name="o_cut", tag="o_cut")
+                part = tile[:, :]
                 o_view = part.rearrange("p (h s q t) -> p s h q t", h=2, s=SETS, q=16, t=4)
                 for n in range(2):
                     acc = new_bank()

@@ -28,7 +28,7 @@ def tile_get_qkv_kernel(tc, x, W, out_0, out_1, out_2):
     with ExitStack() as ctx:
         keep = ctx.enter_context(tc.tile_pool(name="keep", bufs=1))
         rot = ctx.enter_context(tc.tile_pool(name="rot", bufs=3))
-        outp = ctx.enter_context(tc.tile_pool(name="outp", bufs=8))
+        outp = ctx.enter_context(tc.tile_pool(name="outp", bufs=6))
         cutp = ctx.enter_context(tc.tile_pool(name="cutp", bufs=5))
         psum = ctx.enter_context(tc.psum_pool(name="psum", bufs=1))
         ctx.enter_context(tc.manual_schedule())
@@ -47,9 +47,8 @@ def tile_get_qkv_kernel(tc, x, W, out_0, out_1, out_2):
 
         def load_x(i):
             s0, n = (i, 1) if i < 2 else (2 * i - 2, 2)
-            for b in range(2):
-                src = x[b].rearrange("(q s) k -> q (s k)", s=SETS)
-                nc.sync.dma_start(out=x_sb[i][b:P:2, :], in_=src[:, s0 * K:(s0 + n) * K])
+            src = x.rearrange("b (q s) k -> q b (s k)", s=SETS)
+            nc.sync.dma_start(out=x_sb[i][:], in_=src[:, :, s0 * K:(s0 + n) * K])
 
         def x_words(s):
             if s < 2:
@@ -62,18 +61,22 @@ def tile_get_qkv_kernel(tc, x, W, out_0, out_1, out_2):
             for i in range(pieces):
                 w_t = keep.tile([P, n * K], BF16, name="w_sb%d_%d" % (wb, i))
                 nc.sync.dma_start(out=w_t[:], in_=rows[:, i * n * K:(i + 1) * n * K])
-                w_raw[wb] = w_t
+                w_raw[wb] = w_t[:, :]
                 for j in range(n):
                     w_sb[(wb, i * n + j)] = w_t[:].bitcast(F32)[:, j * 512:(j + 1) * 512]
 
         load_x(0)
         load_x(1)
-        load_w(0, 4)
+        load_w(0, 2)
         load_x(2)
         load_x(3)
         load_x(4)
-        for wb in range(1, WBLK):
+        for wb in range(1, WBLK - 2):
             load_w(wb, 1)
+        w_last = keep.tile([P, 2, 4 * K], BF16, name="w_last")
+        nc.sync.dma_start(out=w_last[:], in_=W[(WBLK - 2) * 512:, :].rearrange("(w p t) k -> p w (t k)", w=2, t=4))
+        for i in range(2):
+            w_raw[WBLK - 2 + i] = w_last[:, i, :]
 
         ident = keep.tile([P, P], F32, name="ident")
         make_identity(nc, ident[:])
@@ -119,7 +122,7 @@ def tile_get_qkv_kernel(tc, x, W, out_0, out_1, out_2):
         def order_w(wb):
             wo = rot.tile([P, 2048], F32, name="wo", tag="wo")
             w_ordered[wb] = wo
-            src = w_raw[wb][:].bitcast(F32)
+            src = w_raw[wb].bitcast(F32)
             for h in range(2):
                 nc.vector.tensor_copy(
                     out=wo[:, h * 1024:(h + 1) * 1024].rearrange("p (u c i) -> p c u i", u=2, i=4),
@@ -173,11 +176,16 @@ def tile_get_qkv_kernel(tc, x, W, out_0, out_1, out_2):
             )
 
         o_sb = {}
+        o_first = keep.tile([P, 4096], F32, name="o_first")
 
         def multiply(wb, a, pairs, engines):
             if (wb, a) not in o_sb:
-                o_sb[(wb, a)] = outp.tile([P, 2048], F32, name="o_sb", tag="o_sb")
-            o_view = o_sb[(wb, a)][:].rearrange(
+                if wb == 0:
+                    o_sb[(wb, a)] = o_first[:, a * 2048:(a + 1) * 2048]
+                else:
+                    tile = outp.tile([P, 2048], F32, name="o_sb", tag="o_sb")
+                    o_sb[(wb, a)] = tile[:, :]
+            o_view = o_sb[(wb, a)].rearrange(
                 "p (h s q t) -> p s h q t", h=4, s=SETS, q=16, t=4)
             for n, pair in enumerate(pairs):
                 acc = new_bank()
@@ -188,7 +196,7 @@ def tile_get_qkv_kernel(tc, x, W, out_0, out_1, out_2):
                      acc[:].rearrange("p (i t h q) -> p i h q t", i=2, t=4, h=4, q=16))
 
         def store(wb, a):
-            store_heads(wb, a * 4, 4, o_sb[(wb, a)][:])
+            store_heads(wb, a * 4, 4, o_sb[(wb, a)])
 
         def store_heads(wb, h, heads, tile):
             h0 = (wb % 2) * 8 + h
@@ -236,10 +244,9 @@ def tile_get_qkv_kernel(tc, x, W, out_0, out_1, out_2):
         order_w(1)
         order_w(2)
         multiply(0, 0, [2, 3], [S, S])
-        store(0, 0)
         transpose_w(1, [V, S, V, S])
         multiply(0, 1, [2, 3], [S, S])
-        store(0, 1)
+        store_heads(0, 0, 8, o_first[:, :])
         quantise_w(1, HALVES)
         transpose_w(2, [S, V, S, V])
         for wb in range(1, WBLK):

from contextlib import ExitStack

import concourse.mybir as mybir
from concourse.masks import make_identity

F32 = mybir.dt.float32
BF16 = mybir.dt.bfloat16
U32 = mybir.dt.uint32
U8 = mybir.dt.uint8
FP8X4 = mybir.dt.float8_e4m3fn_x4

P = 128
K = 1024
TOK = 1024
E = 3072
FLOPS = 2 * TOK * K * E

SETS = 8
WBLK = 6
CUT = [(4, 0), (4, 1), (5, 0), (5, 1)]
V = 0
S = 1


def tile_get_qkv_kernel(tc, x, W, out_0, out_1, out_2):
    nc = tc.nc
    outs = [out_0, out_1, out_2]
    with ExitStack() as ctx:
        keep = ctx.enter_context(tc.tile_pool(name="keep", bufs=1))
        rot = ctx.enter_context(tc.tile_pool(name="rot", bufs=3))
        outp = ctx.enter_context(tc.tile_pool(name="outp", bufs=6))
        cutp = ctx.enter_context(tc.tile_pool(name="cutp", bufs=5))
        psum = ctx.enter_context(tc.psum_pool(name="psum", bufs=1))
        ctx.enter_context(tc.manual_schedule())

        counter = [0]

        def new_bank():
            i = counter[0] % 8
            counter[0] += 1
            return psum.tile([P, 512], F32, name="bank%d" % i, tag="bank%d" % i)

        x_sb = [keep.tile([P, K], BF16, name="x_sb%d" % i) for i in range(2)]
        x_sb += [keep.tile([P, 2 * K], BF16, name="x_sb%d" % i) for i in range(2, 5)]
        w_sb = {}
        w_raw = {}

        def load_x(i):
            s0, n = (i, 1) if i < 2 else (2 * i - 2, 2)
            src = x.rearrange("b (q s) k -> q b (s k)", s=SETS)
            nc.sync.dma_start(out=x_sb[i][:], in_=src[:, :, s0 * K:(s0 + n) * K])

        def x_words(s):
            if s < 2:
                return x_sb[s][:].bitcast(F32)
            return x_sb[s // 2 + 1][:].bitcast(F32)[:, (s % 2) * 512:(s % 2 + 1) * 512]

        def load_w(wb, pieces):
            rows = W[wb * 512:(wb + 1) * 512, :].rearrange("(p t) k -> p (t k)", t=4)
            n = 4 // pieces
            for i in range(pieces):
                w_t = keep.tile([P, n * K], BF16, name="w_sb%d_%d" % (wb, i))
                nc.sync.dma_start(out=w_t[:], in_=rows[:, i * n * K:(i + 1) * n * K])
                w_raw[wb] = w_t[:, :]
                for j in range(n):
                    w_sb[(wb, i * n + j)] = w_t[:].bitcast(F32)[:, j * 512:(j + 1) * 512]

        load_x(0)
        load_x(1)
        load_w(0, 2)
        load_x(2)
        load_x(3)
        load_x(4)
        for wb in range(1, WBLK - 2):
            load_w(wb, 1)
        w_last = keep.tile([P, 2, 4 * K], BF16, name="w_last")
        nc.sync.dma_start(out=w_last[:], in_=W[(WBLK - 2) * 512:, :].rearrange("(w p t) k -> p w (t k)", w=2, t=4))
        for i in range(2):
            w_raw[WBLK - 2 + i] = w_last[:, i, :]

        ident = keep.tile([P, P], F32, name="ident")
        make_identity(nc, ident[:])

        xg = [keep.tile([P, 2 * K], BF16, name="xg%d" % i, align_bytes=64) for i in range(4)]
        x_codes = [keep.tile([P, 512], U32, name="x_codes%d" % i, align_bytes=64) for i in range(4)]
        x_scales = [keep.tile([P, 512], U8, name="x_scales%d" % i, align_bytes=64) for i in range(4)]

        def copy(eng, dst, src):
            if eng == V:
                nc.vector.tensor_copy(out=dst, in_=src)
            else:
                nc.scalar.copy(out=dst, in_=src)

        def transpose4(words, ordered):
            bank = new_bank()
            for j in range(4):
                if ordered:
                    w0 = 512 * (j % 2) + P * (j // 2)
                    src = words[:, w0:w0 + P]
                else:
                    w0 = 256 * (j // 2) + j % 2
                    src = words[:, w0:w0 + 255:2]
                nc.tensor.transpose(bank[:, j * P:(j + 1) * P], src, ident[:])
            return bank

        def transpose_x(s, eng):
            bank = transpose4(x_words(s), False)
            dst = xg[s // 2][:].bitcast(F32)[:, (s % 2) * 512:(s % 2 + 1) * 512]
            copy(eng, dst.rearrange("p (g c u) -> p g c u", g=2, u=2),
                 bank[:].rearrange("p (g u c) -> p g c u", g=2, u=2))

        def quantise_x(part):
            nc.vector.quantize_mx(out=x_codes[part][:].bitcast(FP8X4), scales=x_scales[part][:],
                                  in_=xg[part][:])

        w_codes = {}
        w_scales = {}
        w_grouped = {}

        w_ordered = {}

        def order_w(wb):
            wo = rot.tile([P, 2048], F32, name="wo", tag="wo")
            w_ordered[wb] = wo
            src = w_raw[wb].bitcast(F32)
            for h in range(2):
                nc.vector.tensor_copy(
                    out=wo[:, h * 1024:(h + 1) * 1024].rearrange("p (u c i) -> p c u i", u=2, i=4),
                    in_=src[:, h * 1024:(h + 1) * 1024].rearrange("p (c i u) -> p c u i", i=4, u=2))

        def transpose_w(wb, engines):
            wg = rot.tile([P, 4096], BF16, name="wg", tag="wg", align_bytes=64)
            wg32 = wg[:].bitcast(F32).rearrange(
                "p (g a t c u) -> p g a t c u", g=2, a=2, t=4, c=64, u=2)
            wg_cut = wg[:].bitcast(F32).rearrange(
                "p (g a e t c u) -> p g a e t c u", g=2, a=2, e=2, t=4, c=32, u=2)
            for t in range(4):
                if wb in w_ordered:
                    h0 = (t // 2) * 1024 + (t % 2) * 256
                    bank = transpose4(w_ordered[wb][:, h0:h0 + 768], True)
                else:
                    bank = transpose4(w_sb[(wb, t)], False)
                whole = bank[:].rearrange("p (g u a c) -> p g a c u", g=2, u=2, a=2, c=64)
                if (wb, 0) not in CUT and (wb, 1) not in CUT:
                    copy(engines[t], wg32[:, :, :, t, :, :], whole)
                else:
                    cut = bank[:].rearrange("p (g u a e c) -> p g a e c u", g=2, u=2, a=2, e=2, c=32)
                    for a in range(2):
                        if (wb, a) in CUT:
                            copy(engines[t], wg_cut[:, :, a, :, t, :, :], cut[:, :, a, :, :, :])
                        else:
                            copy(engines[t], wg32[:, :, a, t, :, :], whole[:, :, a, :, :])
            w_codes[wb] = rot.tile([P, 1024], U32, name="wc", tag="wc", align_bytes=64)
            w_scales[wb] = rot.tile([P, 1024], U8, name="ws", tag="ws", align_bytes=64)
            w_grouped[wb] = wg

        def quantise_w(wb, q_calls):
            for c0, n in q_calls:
                nc.vector.quantize_mx(
                    out=w_codes[wb][:, c0:c0 + n].bitcast(FP8X4),
                    scales=w_scales[wb][:, c0:c0 + n],
                    in_=w_grouped[wb][:, 4 * c0:4 * (c0 + n)],
                )

        def mx_pass(acc, s, g, wb, col, n):
            off = (s % 2) * 256 + g * P
            c0 = g * 512 + col
            nc.tensor.matmul_mx(
                out=acc,
                lhsT=x_codes[s // 2][:, off:off + P].bitcast(FP8X4),
                lhsT_scale=x_scales[s // 2][:, off:off + P],
                rhs=w_codes[wb][:, c0:c0 + n].bitcast(FP8X4),
                rhs_scale=w_scales[wb][:, c0:c0 + n],
                start=(g == 0),
                stop=(g == 1),
            )

        o_sb = {}
        o_first = keep.tile([P, 4096], F32, name="o_first")

        def multiply(wb, a, pairs, engines):
            if (wb, a) not in o_sb:
                if wb == 0:
                    o_sb[(wb, a)] = o_first[:, a * 2048:(a + 1) * 2048]
                else:
                    tile = outp.tile([P, 2048], F32, name="o_sb", tag="o_sb")
                    o_sb[(wb, a)] = tile[:, :]
            o_view = o_sb[(wb, a)].rearrange(
                "p (h s q t) -> p s h q t", h=4, s=SETS, q=16, t=4)
            for n, pair in enumerate(pairs):
                acc = new_bank()
                for i in range(2):
                    for g in range(2):
                        mx_pass(acc[:, i * 256:(i + 1) * 256], 2 * pair + i, g, wb, a * 256, 256)
                copy(engines[n], o_view[:, 2 * pair:2 * pair + 2, :, :, :],
                     acc[:].rearrange("p (i t h q) -> p i h q t", i=2, t=4, h=4, q=16))

        def store(wb, a):
            store_heads(wb, a * 4, 4, o_sb[(wb, a)])

        def store_heads(wb, h, heads, tile):
            h0 = (wb % 2) * 8 + h
            for b in range(2):
                nc.sync.dma_start(
                    out=outs[wb // 2][b, h0:h0 + heads].rearrange("h (q s) d -> q h (s d)", s=SETS),
                    in_=tile[b:P:2, :])

        def multiply_cut(wb, a, engines):
            for e in range(2):
                tile = cutp.tile([P, 1024], F32, name="o_cut", tag="o_cut")
                part = tile[:, :]
                o_view = part.rearrange("p (h s q t) -> p s h q t", h=2, s=SETS, q=16, t=4)
                for n in range(2):
                    acc = new_bank()
                    for i in range(4):
                        for g in range(2):
                            mx_pass(acc[:, i * P:(i + 1) * P], 4 * n + i, g, wb, a * 256 + e * P, P)
                    copy(engines[2 * e + n], o_view[:, 4 * n:4 * n + 4, :, :, :],
                         acc[:].rearrange("p (i t h q) -> p i h q t", i=4, t=4, h=2, q=16))
                store_heads(wb, a * 4 + 2 * e, 2, part)

        QUARTERS = [(0, 256), (512, 256), (256, 256), (768, 256)]
        HALVES = [(0, 512), (512, 512)]

        transpose_x(0, V)
        transpose_x(1, S)
        quantise_x(0)
        transpose_w(0, [V, S, V, S])
        quantise_w(0, QUARTERS[0:2])
        transpose_x(2, V)
        transpose_x(3, S)
        quantise_w(0, QUARTERS[2:4])
        quantise_x(1)
        transpose_x(4, S)
        transpose_x(5, S)
        multiply(0, 0, [0], [S])
        multiply(0, 1, [0], [S])
        quantise_x(2)
        transpose_x(6, V)
        transpose_x(7, S)
        quantise_x(3)
        multiply(0, 0, [1], [S])
        multiply(0, 1, [1], [S])
        order_w(1)
        order_w(2)
        multiply(0, 0, [2, 3], [S, S])
        transpose_w(1, [V, S, V, S])
        multiply(0, 1, [2, 3], [S, S])
        store_heads(0, 0, 8, o_first[:, :])
        quantise_w(1, HALVES)
        transpose_w(2, [S, V, S, V])
        for wb in range(1, WBLK):
            if wb + 2 < WBLK:
                order_w(wb + 2)
            for a in range(2):
                engines = [S, S, S, S] if wb + 1 < WBLK else [S, V, S, V]
                if (wb, a) in CUT:
                    multiply_cut(wb, a, engines)
                else:
                    multiply(wb, a, [0, 1, 2, 3], engines)
                    store(wb, a)
                if a == 0 and wb + 1 < WBLK:
                    quantise_w(wb + 1, HALVES)
            if wb + 2 < WBLK:
                transpose_w(wb + 2, [V, V, V, V])
